import numpy as np
import ml_dtypes


def mxq(x, axis, fmt="e4m3"):
    dtype, down = {"e4m3": (ml_dtypes.float8_e4m3fn, 7), "e5m2": (ml_dtypes.float8_e5m2, 14)}[fmt]
    v = np.moveaxis(np.asarray(x, np.float32).astype(ml_dtypes.bfloat16).astype(np.float64), axis, -1)
    blocks = v.reshape(v.shape[:-1] + (-1, 32))
    amax = np.abs(blocks).max(-1, keepdims=True)
    byte = np.maximum(np.where(amax > 0, np.frexp(amax)[1] - 1 + 127, 0) - down, 1)
    scale = np.exp2(byte - 127.0)
    codes = (blocks / scale).astype(np.float32).astype(dtype).astype(np.float64)
    return np.moveaxis((codes * scale).reshape(v.shape), -1, axis)


WIDE = False


def mx_kscale(k):
    if not WIDE:
        return np.ones(k)
    levels = np.array([10, -10, 5, -5, 0])
    if k % 512:
        return np.exp2(np.random.permutation(np.resize(levels, k // 32))).repeat(32)
    a = np.empty((k // 512, 16))
    for p in range(k // 512):
        a[p, :8] = np.random.permutation(np.resize(levels, 8))
        for g in range(8):
            far = levels[np.abs(levels - a[p, g]) >= 10]
            a[p, g + 8] = far[np.random.randint(len(far))]
    return np.exp2(a.ravel()).repeat(32)


BF16 = ml_dtypes.bfloat16


def bf(x):
    return np.asarray(x, np.float32).astype(BF16)


def f64(x):
    return np.asarray(x).astype(np.float64)


SL, BS, DM, H, NH, DO = 128, 128, 512, 8, 64, 256
DP = H * NH


def setup_inputs():
    s, t = mx_kscale(DM), mx_kscale(DP)
    g = np.random.standard_normal((SL, BS, H)) * 2.0
    return {"values": bf(np.random.standard_normal((SL, BS, DM)) * s),
            "logw": bf(g - np.log(np.exp(g).sum(0, keepdims=True))),
            "Wv": bf(np.random.standard_normal((DP, DM)) / np.sqrt(DM * SL) / s * t[:, None]),
            "Wo": bf(np.random.standard_normal((DO, DP)) * 0.5 / np.sqrt(DP) / t)}


def reference(values, logw, Wv, Wo):
    vp = mxq(f64(values), 2, "e4m3") @ mxq(f64(Wv), 1, "e4m3").T
    attn = (f64(logw)[..., None] * vp.reshape(SL, BS, H, NH)).sum(0)
    return mxq(attn.reshape(BS, DP), 1, "e4m3") @ mxq(f64(Wo), 1, "e4m3").T

@@ -1,0 +1,245 @@
+import concourse.mybir as mybir
+from concourse.masks import make_identity
+
+F32 = mybir.dt.float32
+BF16 = mybir.dt.bfloat16
+U32 = mybir.dt.uint32
+U8 = mybir.dt.uint8
+FP8X4 = mybir.dt.float8_e4m3fn_x4
+MULT = mybir.AluOpType.mult
+ADD = mybir.AluOpType.add
+COPY = mybir.ActivationFunctionType.Copy
+
+P = 128
+SL, BS, DM, H, NH, DO = 128, 128, 512, 8, 64, 256
+DP = H * NH
+PACK = 4
+PAIRS = DM // 2
+GROUP = 4
+N_GROUPS = SL // GROUP
+SCALAR_EVERY = 3
+WO_ROUND = 3
+
+FLOPS = 2 * SL * BS * DM * DP + 2 * BS * DP * DO
+
+
+def tile_multiheadattention_pb_t_kernel(tc, values, logw, Wv, Wo, out):
+    nc = tc.nc
+    with tc.tile_pool(name="const", bufs=1) as const, tc.tile_pool(
+        name="rows", bufs=N_GROUPS
+    ) as rows_pool, tc.tile_pool(name="work", bufs=3) as work_pool, tc.tile_pool(
+        name="prod", bufs=4
+    ) as prod_pool, tc.psum_pool(name="flip", bufs=2) as flip_pool, tc.psum_pool(
+        name="proj", bufs=5
+    ) as proj_pool, tc.psum_pool(name="sum", bufs=1) as sum_pool, tc.manual_schedule():
+        wv_rows = const.tile([P, 4 * DM], BF16)
+        nc.sync.dma_start(
+            out=wv_rows[:].rearrange("p (t k) -> p t k", k=DM),
+            in_=Wv.rearrange("(p t) k -> p t k", p=P),
+        )
+        logw_rows = const.tile([P, BS * H], BF16)
+        nc.scalar.dma_start(out=logw_rows[:], in_=logw.rearrange("s b h -> s (b h)"))
+        wo_rows = const.tile([P, 2, DP], BF16)
+        nc.scalar.dma_start(out=wo_rows[:], in_=Wo.rearrange("(i p) c -> p i c", p=P))
+        value_rows = []
+        for g in range(N_GROUPS):
+            rows = rows_pool.tile([P, GROUP * DM], BF16)
+            nc.sync.dma_start(
+                out=rows[:].rearrange("b (s k) -> b s k", k=DM),
+                in_=values[g * GROUP : (g + 1) * GROUP].rearrange("s b k -> b s k"),
+            )
+            value_rows.append(rows)
+
+        ident = const.tile([P, P], F32)
+        make_identity(nc, ident[:])
+
+        def pairs_onto_partitions(src_pairs, dst_pairs):
+            bank = flip_pool.tile([P, 2, 2, P], F32, tag="flip")
+            for blk in range(2):
+                for u in range(2):
+                    nc.tensor.transpose(
+                        bank[:, blk, u, :], src_pairs[:, blk, u:PAIRS:2], ident[:]
+                    )
+            nc.scalar.copy(out=dst_pairs, in_=bank[:].rearrange("p k u r -> p k r u"))
+
+        logw_by_head = const.tile([P, H, BS], F32)
+        nc.vector.tensor_copy(
+            out=logw_by_head[:], in_=logw_rows[:].rearrange("s (b h) -> s h b", h=H)
+        )
+
+        wv_grouped = const.tile([P, DP * PACK], BF16, align_bytes=64)
+        wv_codes = const.tile([P, DP], U32, align_bytes=64)
+        wv_scales = const.tile([P, DP], U8, align_bytes=64)
+        wv_pairs = wv_rows[:].bitcast(F32).rearrange("p (t w) -> p t w", w=PAIRS)
+        wv_grouped_pairs = wv_grouped[:].bitcast(F32).rearrange("p (t c u) -> p t c u", c=P, u=2)
+        for half in range(2):
+            pairs_onto_partitions(
+                wv_pairs[:, 2 * half : 2 * half + 2, :],
+                wv_grouped_pairs[:, 2 * half : 2 * half + 2, :, :],
+            )
+        nc.vector.quantize_mx(
+            out=wv_codes[:].bitcast(FP8X4), scales=wv_scales[:], in_=wv_grouped[:]
+        )
+
+        weight = const.tile([P, H, SL], F32)
+
+        def transpose_logw():
+            for half in range(2):
+                bank = flip_pool.tile([P, H // 2, SL], F32, tag="flip")
+                for i in range(H // 2):
+                    nc.tensor.transpose(
+                        bank[:, i, :], logw_by_head[:, half * (H // 2) + i, :], ident[:]
+                    )
+                nc.scalar.copy(
+                    out=weight[:, half * (H // 2) : (half + 1) * (H // 2), :], in_=bank[:]
+                )
+
+        wo_grouped = const.tile([P, DO * PACK], BF16, align_bytes=64)
+        wo_codes = const.tile([P, DO], U32, align_bytes=64)
+        wo_scales = const.tile([P, DO], U8, align_bytes=64)
+
+        def transpose_wo():
+            pairs_onto_partitions(
+                wo_rows[:].rearrange("p i c -> p (i c)").bitcast(F32).rearrange("p (i w) -> p i w", w=PAIRS),
+                wo_grouped[:].bitcast(F32).rearrange("p (i o u) -> p i o u", o=P, u=2),
+            )
+
+        def quantise_wo():
+            nc.vector.quantize_mx(
+                out=wo_codes[:].bitcast(FP8X4),
+                scales=wo_scales[:],
+                in_=wo_grouped[:],
+            )
+
+        grouped_of = {}
+        codes_of = {}
+        scales_of = {}
+        proj_of = {}
+        product_of = {}
+
+        def transpose_group(g):
+            grouped = work_pool.tile([P, GROUP * BS * PACK], BF16, align_bytes=64)
+            src = value_rows[g][:].bitcast(F32).rearrange("b (s w) -> b s w", w=PAIRS)
+            dst = grouped[:].bitcast(F32).rearrange("p (s b u) -> p s b u", b=BS, u=2)
+            for half in range(GROUP // 2):
+                pairs_onto_partitions(
+                    src[:, 2 * half : 2 * half + 2, :], dst[:, 2 * half : 2 * half + 2, :, :]
+                )
+            grouped_of[g] = grouped
+
+        def quantise_group(g):
+            codes = work_pool.tile([P, GROUP * BS], U32, align_bytes=64)
+            scales = work_pool.tile([P, GROUP * BS], U8, align_bytes=64)
+            nc.vector.quantize_mx(
+                out=codes[:].bitcast(FP8X4), scales=scales[:], in_=grouped_of[g][:]
+            )
+            codes_of[g] = codes
+            scales_of[g] = scales
+
+        def project_group(g):
+            for j in range(GROUP):
+                batch = slice(j * BS, (j + 1) * BS)
+                proj = proj_pool.tile([P, DP], F32)
+                nc.tensor.matmul_mx(
+                    out=proj[:],
+                    lhsT=codes_of[g][:, batch].bitcast(FP8X4),
+                    lhsT_scale=scales_of[g][:, batch],
+                    rhs=wv_codes[:].bitcast(FP8X4),
+                    rhs_scale=wv_scales[:],
+                    start=True,
+                    stop=True,
+                )
+                proj_of[g * GROUP + j] = proj
+
+        def by_scalar(s):
+            return s % SCALAR_EVERY == SCALAR_EVERY - 1
+
+        attn_part = const.tile([P, DP], F32)
+        nc.vector.memset(attn_part[:], 0.0)
+
+        def head_columns(tile, h):
+            return tile[:].rearrange("b (t h i) -> b h t i", t=PACK, h=H)[:, h]
+
+        def pool_group(g):
+            for s in range(g * GROUP, (g + 1) * GROUP):
+                if by_scalar(s):
+                    product = prod_pool.tile([P, DP], F32)
+                    product_of[s] = product
+                for h in range(H):
+                    if by_scalar(s):
+                        nc.scalar.activation(
+                            out=head_columns(product, h),
+                            in_=head_columns(proj_of[s], h),
+                            func=COPY,
+                            scale=weight[:, h, s : s + 1],
+                        )
+                    else:
+                        nc.vector.scalar_tensor_tensor(
+                            out=head_columns(attn_part, h),
+                            in0=head_columns(proj_of[s], h),
+                            scalar=weight[:, h, s : s + 1],
+                            in1=head_columns(attn_part, h),
+                            op0=MULT,
+                            op1=ADD,
+                        )
+
+        attn_sum = sum_pool.tile([P, PACK, BS], F32)
+
+        def add_transposed(term, first, last):
+            for t in range(PACK):
+                nc.tensor.matmul(
+                    out=attn_sum[:, t, :],
+                    lhsT=term[:, t * P : (t + 1) * P],
+                    rhs=ident[:],
+                    is_transpose=True,
+                    start=first and t == 0,
+                    stop=last and t == PACK - 1,
+                )
+
+        def add_products_of_group(g):
+            for s in range(g * GROUP, (g + 1) * GROUP):
+                if by_scalar(s):
+                    add_transposed(product_of[s], first=(s == SCALAR_EVERY - 1), last=False)
+
+        transpose_group(0)
+        transpose_logw()
+        transpose_group(1)
+        for g in range(1, N_GROUPS + 3):
+            if g <= N_GROUPS:
+                quantise_group(g - 1)
+            if g == WO_ROUND + 1:
+                quantise_wo()
+            if 2 <= g <= N_GROUPS + 1:
+                pool_group(g - 2)
+            if g + 1 < N_GROUPS:
+                transpose_group(g + 1)
+            if g >= 3:
+                add_products_of_group(g - 3)
+            if g == WO_ROUND:
+                transpose_wo()
+            if g <= N_GROUPS:
+                project_group(g - 1)
+
+        add_transposed(attn_part, first=False, last=True)
+        attn_grouped = const.tile([P, BS, PACK], BF16, align_bytes=64)
+        nc.scalar.copy(out=attn_grouped[:], in_=attn_sum[:].rearrange("p t b -> p b t"))
+        attn_codes = const.tile([P, BS], U32, align_bytes=64)
+        attn_scales = const.tile([P, BS], U8, align_bytes=64)
+        nc.vector.quantize_mx(
+            out=attn_codes[:].bitcast(FP8X4),
+            scales=attn_scales[:],
+            in_=attn_grouped[:].rearrange("p b t -> p (b t)"),
+        )
+        out_bank = flip_pool.tile([P, DO], F32, tag="flip")
+        nc.tensor.matmul_mx(
+            out=out_bank[:],
+            lhsT=attn_codes[:].bitcast(FP8X4),
+            lhsT_scale=attn_scales[:],
+            rhs=wo_codes[:].bitcast(FP8X4),
+            rhs_scale=wo_scales[:],
+            start=True,
+            stop=True,
+        )
+        out_rows = const.tile([P, DO], F32)
+        nc.vector.tensor_copy(out=out_rows[:], in_=out_bank[:])
+        nc.sync.dma_start(out=out, in_=out_rows[:])

@@ -28,9 +28,9 @@ def tile_multiheadattention_pb_t_kernel(tc, values, logw, Wv, Wo, out):
     with tc.tile_pool(name="const", bufs=1) as const, tc.tile_pool(
         name="rows", bufs=N_GROUPS
     ) as rows_pool, tc.tile_pool(name="work", bufs=3) as work_pool, tc.tile_pool(
-        name="prod", bufs=4
-    ) as prod_pool, tc.psum_pool(name="flip", bufs=2) as flip_pool, tc.psum_pool(
-        name="proj", bufs=5
+        name="prod", bufs=6
+    ) as prod_pool, tc.psum_pool(name="flip", bufs=3) as flip_pool, tc.psum_pool(
+        name="proj", bufs=4
     ) as proj_pool, tc.psum_pool(name="sum", bufs=1) as sum_pool, tc.manual_schedule():
         wv_rows = const.tile([P, 4 * DM], BF16)
         nc.sync.dma_start(
@@ -196,10 +196,24 @@ def tile_multiheadattention_pb_t_kernel(tc, values, logw, Wv, Wo, out):
                     stop=last and t == PACK - 1,
                 )
 
+        attn_side = const.tile([P, DP], F32)
+        nc.gpsimd.memset(attn_side[:], 0.0)
+
         def add_products_of_group(g):
             for s in range(g * GROUP, (g + 1) * GROUP):
-                if by_scalar(s):
+                if not by_scalar(s):
+                    continue
+                if s // SCALAR_EVERY % 2 == 0:
                     add_transposed(product_of[s], first=(s == SCALAR_EVERY - 1), last=False)
+                else:
+                    for t in range(PACK):
+                        cols = slice(t * P, (t + 1) * P)
+                        nc.gpsimd.tensor_tensor(
+                            out=attn_side[:, cols],
+                            in0=attn_side[:, cols],
+                            in1=product_of[s][:, cols],
+                            op=ADD,
+                        )
 
         transpose_group(0)
         transpose_logw()
@@ -220,6 +234,7 @@ def tile_multiheadattention_pb_t_kernel(tc, values, logw, Wv, Wo, out):
             if g <= N_GROUPS:
                 project_group(g - 1)
 
+        add_transposed(attn_side, first=False, last=False)
         add_transposed(attn_part, first=False, last=True)
         attn_grouped = const.tile([P, BS, PACK], BF16, align_bytes=64)
         nc.scalar.copy(out=attn_grouped[:], in_=attn_sum[:].rearrange("p t b -> p b t"))

@@ -18,6 +18,7 @@ PAIRS = DM // 2
 GROUP = 4
 N_GROUPS = SL // GROUP
 SCALAR_EVERY = 3
+LAST_GROUPS = 1
 WO_ROUND = 3
 
 FLOPS = 2 * SL * BS * DM * DP + 2 * BS * DP * DO
@@ -33,39 +34,52 @@ def tile_multiheadattention_pb_t_kernel(tc, values, logw, Wv, Wo, out):
         name="proj", bufs=4
     ) as proj_pool, tc.psum_pool(name="sum", bufs=1) as sum_pool, tc.manual_schedule():
         wv_rows = const.tile([P, 4 * DM], BF16)
-        nc.sync.dma_start(
-            out=wv_rows[:].rearrange("p (t k) -> p t k", k=DM),
-            in_=Wv.rearrange("(p t) k -> p t k", p=P),
-        )
-        logw_rows = const.tile([P, BS * H], BF16)
-        nc.scalar.dma_start(out=logw_rows[:], in_=logw.rearrange("s b h -> s (b h)"))
-        wo_rows = const.tile([P, 2, DP], BF16)
-        nc.scalar.dma_start(out=wo_rows[:], in_=Wo.rearrange("(i p) c -> p i c", p=P))
+        wv_rows_of = wv_rows[:].rearrange("p (t k) -> p t k", k=DM)
+        for half in range(2):
+            nc.sync.dma_start(
+                out=wv_rows_of[:, 2 * half : 2 * half + 2, :],
+                in_=Wv.rearrange("(p t) k -> p t k", p=P)[:, 2 * half : 2 * half + 2, :],
+            )
         value_rows = []
+        logw_rows = const.tile([P, BS * H], BF16)
+        wo_rows = const.tile([P, 2, DP], BF16)
         for g in range(N_GROUPS):
             rows = rows_pool.tile([P, GROUP * DM], BF16)
-            nc.sync.dma_start(
-                out=rows[:].rearrange("b (s k) -> b s k", k=DM),
-                in_=values[g * GROUP : (g + 1) * GROUP].rearrange("s b k -> b s k"),
-            )
+            rows_of = rows[:].rearrange("b (s k) -> b s k", k=DM)
+            pieces = 2 if g == 0 else 1
+            n = GROUP // pieces
+            for i in range(pieces):
+                nc.sync.dma_start(
+                    out=rows_of[:, i * n : (i + 1) * n, :],
+                    in_=values[g * GROUP + i * n : g * GROUP + (i + 1) * n].rearrange(
+                        "s b k -> b s k"
+                    ),
+                )
+            if g == 0:
+                nc.sync.dma_start(out=logw_rows[:], in_=logw.rearrange("s b h -> s (b h)"))
+            if g == WO_ROUND:
+                nc.sync.dma_start(out=wo_rows[:], in_=Wo.rearrange("(i p) c -> p i c", p=P))
             value_rows.append(rows)
 
         ident = const.tile([P, P], F32)
         make_identity(nc, ident[:])
 
-        def pairs_onto_partitions(src_pairs, dst_pairs):
+        def copy_by_scalar(out, in_):
+            nc.scalar.copy(out=out, in_=in_)
+
+        def copy_by_vector(out, in_):
+            nc.vector.tensor_copy(out=out, in_=in_)
+
+        in_turn = (copy_by_scalar, copy_by_vector)
+
+        def pairs_onto_partitions(src_pairs, dst_pairs, copy=copy_by_scalar):
             bank = flip_pool.tile([P, 2, 2, P], F32, tag="flip")
             for blk in range(2):
                 for u in range(2):
                     nc.tensor.transpose(
                         bank[:, blk, u, :], src_pairs[:, blk, u:PAIRS:2], ident[:]
                     )
-            nc.scalar.copy(out=dst_pairs, in_=bank[:].rearrange("p k u r -> p k r u"))
-
-        logw_by_head = const.tile([P, H, BS], F32)
-        nc.vector.tensor_copy(
-            out=logw_by_head[:], in_=logw_rows[:].rearrange("s (b h) -> s h b", h=H)
-        )
+            copy(out=dst_pairs, in_=bank[:].rearrange("p k u r -> p k r u"))
 
         wv_grouped = const.tile([P, DP * PACK], BF16, align_bytes=64)
         wv_codes = const.tile([P, DP], U32, align_bytes=64)
@@ -76,23 +90,36 @@ def tile_multiheadattention_pb_t_kernel(tc, values, logw, Wv, Wo, out):
             pairs_onto_partitions(
                 wv_pairs[:, 2 * half : 2 * half + 2, :],
                 wv_grouped_pairs[:, 2 * half : 2 * half + 2, :, :],
+                in_turn[half],
             )
-        nc.vector.quantize_mx(
-            out=wv_codes[:].bitcast(FP8X4), scales=wv_scales[:], in_=wv_grouped[:]
-        )
+
+        def quantise_wv():
+            nc.vector.quantize_mx(
+                out=wv_codes[:].bitcast(FP8X4), scales=wv_scales[:], in_=wv_grouped[:]
+            )
 
         weight = const.tile([P, H, SL], F32)
 
+        logw_by_head = const.tile([P, H, BS], F32)
+        for h in range(0, H, 2):
+            nc.gpsimd.tensor_scalar(
+                out=logw_by_head[:, h : h + 2, :],
+                in0=logw_rows[:].rearrange("s (b h) -> s h b", h=H)[:, h : h + 2, :],
+                scalar1=1.0,
+                scalar2=0.0,
+                op0=MULT,
+                op1=ADD,
+            )
+
         def transpose_logw():
             for half in range(2):
+                heads = slice(half * (H // 2), (half + 1) * (H // 2))
                 bank = flip_pool.tile([P, H // 2, SL], F32, tag="flip")
                 for i in range(H // 2):
                     nc.tensor.transpose(
                         bank[:, i, :], logw_by_head[:, half * (H // 2) + i, :], ident[:]
                     )
-                nc.scalar.copy(
-                    out=weight[:, half * (H // 2) : (half + 1) * (H // 2), :], in_=bank[:]
-                )
+                in_turn[1 - half](out=weight[:, heads, :], in_=bank[:])
 
         wo_grouped = const.tile([P, DO * PACK], BF16, align_bytes=64)
         wo_codes = const.tile([P, DO], U32, align_bytes=64)
@@ -123,7 +150,8 @@ def tile_multiheadattention_pb_t_kernel(tc, values, logw, Wv, Wo, out):
             dst = grouped[:].bitcast(F32).rearrange("p (s b u) -> p s b u", b=BS, u=2)
             for half in range(GROUP // 2):
                 pairs_onto_partitions(
-                    src[:, 2 * half : 2 * half + 2, :], dst[:, 2 * half : 2 * half + 2, :, :]
+                    src[:, 2 * half : 2 * half + 2, :],
+                    dst[:, 2 * half : 2 * half + 2, :, :],
                 )
             grouped_of[g] = grouped
 
@@ -151,37 +179,45 @@ def tile_multiheadattention_pb_t_kernel(tc, values, logw, Wv, Wo, out):
                 )
                 proj_of[g * GROUP + j] = proj
 
-        def by_scalar(s):
-            return s % SCALAR_EVERY == SCALAR_EVERY - 1
-
         attn_part = const.tile([P, DP], F32)
         nc.vector.memset(attn_part[:], 0.0)
 
         def head_columns(tile, h):
             return tile[:].rearrange("b (t h i) -> b h t i", t=PACK, h=H)[:, h]
 
-        def pool_group(g):
+        def by_scalar(s):
+            return s % SCALAR_EVERY == SCALAR_EVERY - 1
+
+        def by_gpsimd(s):
+            return s // SCALAR_EVERY % 2 == 1 and s < SL - LAST_GROUPS * GROUP
+
+        def multiply_group(g):
             for s in range(g * GROUP, (g + 1) * GROUP):
-                if by_scalar(s):
-                    product = prod_pool.tile([P, DP], F32)
-                    product_of[s] = product
+                if not by_scalar(s):
+                    continue
+                product = prod_pool.tile([P, DP], F32)
+                product_of[s] = product
                 for h in range(H):
-                    if by_scalar(s):
-                        nc.scalar.activation(
-                            out=head_columns(product, h),
-                            in_=head_columns(proj_of[s], h),
-                            func=COPY,
-                            scale=weight[:, h, s : s + 1],
-                        )
-                    else:
-                        nc.vector.scalar_tensor_tensor(
-                            out=head_columns(attn_part, h),
-                            in0=head_columns(proj_of[s], h),
-                            scalar=weight[:, h, s : s + 1],
-                            in1=head_columns(attn_part, h),
-                            op0=MULT,
-                            op1=ADD,
-                        )
+                    nc.scalar.activation(
+                        out=head_columns(product, h),
+                        in_=head_columns(proj_of[s], h),
+                        func=COPY,
+                        scale=weight[:, h, s : s + 1],
+                    )
+
+        def pool_steps(steps):
+            for s in steps:
+                if by_scalar(s):
+                    continue
+                for h in range(H):
+                    nc.vector.scalar_tensor_tensor(
+                        out=head_columns(attn_part, h),
+                        in0=head_columns(proj_of[s], h),
+                        scalar=weight[:, h, s : s + 1],
+                        in1=head_columns(attn_part, h),
+                        op0=MULT,
+                        op1=ADD,
+                    )
 
         attn_sum = sum_pool.tile([P, PACK, BS], F32)
 
@@ -203,7 +239,7 @@ def tile_multiheadattention_pb_t_kernel(tc, values, logw, Wv, Wo, out):
             for s in range(g * GROUP, (g + 1) * GROUP):
                 if not by_scalar(s):
                     continue
-                if s // SCALAR_EVERY % 2 == 0:
+                if not by_gpsimd(s):
                     add_transposed(product_of[s], first=(s == SCALAR_EVERY - 1), last=False)
                 else:
                     for t in range(PACK):
@@ -216,15 +252,26 @@ def tile_multiheadattention_pb_t_kernel(tc, values, logw, Wv, Wo, out):
                         )
 
         transpose_group(0)
+        quantise_wv()
         transpose_logw()
+        quantise_group(0)
         transpose_group(1)
-        for g in range(1, N_GROUPS + 3):
+        project_group(0)
+        for g in range(2, N_GROUPS + 3):
+            pooled = range((g - 2) * GROUP, (g - 1) * GROUP)
+            if g < N_GROUPS + 2:
+                multiply_group(g - 2)
+                if g == 2:
+                    pool_steps(pooled[:1])
+                    pooled = pooled[1:]
             if g <= N_GROUPS:
                 quantise_group(g - 1)
-            if g == WO_ROUND + 1:
+            if g == WO_ROUND + 2:
                 quantise_wo()
-            if 2 <= g <= N_GROUPS + 1:
-                pool_group(g - 2)
+            if g < N_GROUPS + 2:
+                pool_steps(pooled)
+            if g == 2:
+                transpose_group(g)
             if g + 1 < N_GROUPS:
                 transpose_group(g + 1)
             if g >= 3:

@@ -19,6 +19,15 @@ GROUP = 4
 N_GROUPS = SL // GROUP
 SCALAR_EVERY = 3
 LAST_GROUPS = 1
+FIRST_PART = 8
+PART = 16
+
+
+def logw_part(j):
+    return max(0, FIRST_PART + (j - 1) * PART), min(SL, FIRST_PART + j * PART)
+
+
+N_PARTS = 1 + (SL - FIRST_PART + PART - 1) // PART
 WO_ROUND = 3
 
 FLOPS = 2 * SL * BS * DM * DP + 2 * BS * DP * DO
@@ -40,8 +49,16 @@ def tile_multiheadattention_pb_t_kernel(tc, values, logw, Wv, Wo, out):
                 out=wv_rows_of[:, 2 * half : 2 * half + 2, :],
                 in_=Wv.rearrange("(p t) k -> p t k", p=P)[:, 2 * half : 2 * half + 2, :],
             )
+        logw_rows = const.tile([P, SL, 2 * H], BF16)
+
+        def load_logw(j):
+            first, last = logw_part(j)
+            nc.sync.dma_start(
+                out=logw_rows[:, first:last, :H],
+                in_=logw[first:last].rearrange("s b h -> b s h"),
+            )
+
         value_rows = []
-        logw_rows = const.tile([P, BS * H], BF16)
         wo_rows = const.tile([P, 2, DP], BF16)
         for g in range(N_GROUPS):
             rows = rows_pool.tile([P, GROUP * DM], BF16)
@@ -55,8 +72,8 @@ def tile_multiheadattention_pb_t_kernel(tc, values, logw, Wv, Wo, out):
                         "s b k -> b s k"
                     ),
                 )
-            if g == 0:
-                nc.sync.dma_start(out=logw_rows[:], in_=logw.rearrange("s b h -> s (b h)"))
+            if g % 2 == 0 and g // 2 < N_PARTS:
+                load_logw(g // 2)
             if g == WO_ROUND:
                 nc.sync.dma_start(out=wo_rows[:], in_=Wo.rearrange("(i p) c -> p i c", p=P))
             value_rows.append(rows)
@@ -98,28 +115,20 @@ def tile_multiheadattention_pb_t_kernel(tc, values, logw, Wv, Wo, out):
                 out=wv_codes[:].bitcast(FP8X4), scales=wv_scales[:], in_=wv_grouped[:]
             )
 
-        weight = const.tile([P, H, SL], F32)
+        weight = const.tile([P, SL, H], F32)
 
-        logw_by_head = const.tile([P, H, BS], F32)
-        for h in range(0, H, 2):
+        def widen_logw(j):
+            first, last = logw_part(j)
             nc.gpsimd.tensor_scalar(
-                out=logw_by_head[:, h : h + 2, :],
-                in0=logw_rows[:].rearrange("s (b h) -> s h b", h=H)[:, h : h + 2, :],
+                out=weight[:, first:last, :],
+                in0=logw_rows[:, first:last, :H],
                 scalar1=1.0,
                 scalar2=0.0,
                 op0=MULT,
                 op1=ADD,
             )
 
-        def transpose_logw():
-            for half in range(2):
-                heads = slice(half * (H // 2), (half + 1) * (H // 2))
-                bank = flip_pool.tile([P, H // 2, SL], F32, tag="flip")
-                for i in range(H // 2):
-                    nc.tensor.transpose(
-                        bank[:, i, :], logw_by_head[:, half * (H // 2) + i, :], ident[:]
-                    )
-                in_turn[1 - half](out=weight[:, heads, :], in_=bank[:])
+        widen_logw(0)
 
         wo_grouped = const.tile([P, DO * PACK], BF16, align_bytes=64)
         wo_codes = const.tile([P, DO], U32, align_bytes=64)
@@ -202,7 +211,7 @@ def tile_multiheadattention_pb_t_kernel(tc, values, logw, Wv, Wo, out):
                         out=head_columns(product, h),
                         in_=head_columns(proj_of[s], h),
                         func=COPY,
-                        scale=weight[:, h, s : s + 1],
+                        scale=weight[:, s, h : h + 1],
                     )
 
         def pool_steps(steps):
@@ -213,7 +222,7 @@ def tile_multiheadattention_pb_t_kernel(tc, values, logw, Wv, Wo, out):
                     nc.vector.scalar_tensor_tensor(
                         out=head_columns(attn_part, h),
                         in0=head_columns(proj_of[s], h),
-                        scalar=weight[:, h, s : s + 1],
+                        scalar=weight[:, s, h : h + 1],
                         in1=head_columns(attn_part, h),
                         op0=MULT,
                         op1=ADD,
@@ -253,12 +262,13 @@ def tile_multiheadattention_pb_t_kernel(tc, values, logw, Wv, Wo, out):
 
         transpose_group(0)
         quantise_wv()
-        transpose_logw()
         quantise_group(0)
         transpose_group(1)
         project_group(0)
         for g in range(2, N_GROUPS + 3):
             pooled = range((g - 2) * GROUP, (g - 1) * GROUP)
+            if g % 4 == 2 and (g + 2) // 4 < N_PARTS:
+                widen_logw((g + 2) // 4)
             if g < N_GROUPS + 2:
                 multiply_group(g - 2)
                 if g == 2:

import concourse.mybir as mybir
from concourse.masks import make_identity

F32 = mybir.dt.float32
BF16 = mybir.dt.bfloat16
U32 = mybir.dt.uint32
U8 = mybir.dt.uint8
FP8X4 = mybir.dt.float8_e4m3fn_x4
MULT = mybir.AluOpType.mult
ADD = mybir.AluOpType.add
COPY = mybir.ActivationFunctionType.Copy

P = 128
SL, BS, DM, H, NH, DO = 128, 128, 512, 8, 64, 256
DP = H * NH
PACK = 4
PAIRS = DM // 2
GROUP = 4
N_GROUPS = SL // GROUP
SCALAR_EVERY = 3
LAST_GROUPS = 1
FIRST_PART = 8
PART = 16


def logw_part(j):
    return max(0, FIRST_PART + (j - 1) * PART), min(SL, FIRST_PART + j * PART)


N_PARTS = 1 + (SL - FIRST_PART + PART - 1) // PART
WO_ROUND = 3

FLOPS = 2 * SL * BS * DM * DP + 2 * BS * DP * DO


def tile_multiheadattention_pb_t_kernel(tc, values, logw, Wv, Wo, out):
    nc = tc.nc
    with tc.tile_pool(name="const", bufs=1) as const, tc.tile_pool(
        name="rows", bufs=N_GROUPS
    ) as rows_pool, tc.tile_pool(name="work", bufs=3) as work_pool, tc.tile_pool(
        name="prod", bufs=6
    ) as prod_pool, tc.psum_pool(name="flip", bufs=3) as flip_pool, tc.psum_pool(
        name="proj", bufs=4
    ) as proj_pool, tc.psum_pool(name="sum", bufs=1) as sum_pool, tc.manual_schedule():
        wv_rows = const.tile([P, 4 * DM], BF16)
        wv_rows_of = wv_rows[:].rearrange("p (t k) -> p t k", k=DM)
        for half in range(2):
            nc.sync.dma_start(
                out=wv_rows_of[:, 2 * half : 2 * half + 2, :],
                in_=Wv.rearrange("(p t) k -> p t k", p=P)[:, 2 * half : 2 * half + 2, :],
            )
        logw_rows = const.tile([P, SL, 2 * H], BF16)

        def load_logw(j):
            first, last = logw_part(j)
            nc.sync.dma_start(
                out=logw_rows[:, first:last, :H],
                in_=logw[first:last].rearrange("s b h -> b s h"),
            )

        value_rows = []
        wo_rows = const.tile([P, 2, DP], BF16)
        for g in range(N_GROUPS):
            rows = rows_pool.tile([P, GROUP * DM], BF16)
            rows_of = rows[:].rearrange("b (s k) -> b s k", k=DM)
            pieces = 2 if g == 0 else 1
            n = GROUP // pieces
            for i in range(pieces):
                nc.sync.dma_start(
                    out=rows_of[:, i * n : (i + 1) * n, :],
                    in_=values[g * GROUP + i * n : g * GROUP + (i + 1) * n].rearrange(
                        "s b k -> b s k"
                    ),
                )
            if g % 2 == 0 and g // 2 < N_PARTS:
                load_logw(g // 2)
            if g == WO_ROUND:
                nc.sync.dma_start(out=wo_rows[:], in_=Wo.rearrange("(i p) c -> p i c", p=P))
            value_rows.append(rows)

        ident = const.tile([P, P], F32)
        make_identity(nc, ident[:])

        def copy_by_scalar(out, in_):
            nc.scalar.copy(out=out, in_=in_)

        def copy_by_vector(out, in_):
            nc.vector.tensor_copy(out=out, in_=in_)

        in_turn = (copy_by_scalar, copy_by_vector)

        def pairs_onto_partitions(src_pairs, dst_pairs, copy=copy_by_scalar):
            bank = flip_pool.tile([P, 2, 2, P], F32, tag="flip")
            for blk in range(2):
                for u in range(2):
                    nc.tensor.transpose(
                        bank[:, blk, u, :], src_pairs[:, blk, u:PAIRS:2], ident[:]
                    )
            copy(out=dst_pairs, in_=bank[:].rearrange("p k u r -> p k r u"))

        wv_grouped = const.tile([P, DP * PACK], BF16, align_bytes=64)
        wv_codes = const.tile([P, DP], U32, align_bytes=64)
        wv_scales = const.tile([P, DP], U8, align_bytes=64)
        wv_pairs = wv_rows[:].bitcast(F32).rearrange("p (t w) -> p t w", w=PAIRS)
        wv_grouped_pairs = wv_grouped[:].bitcast(F32).rearrange("p (t c u) -> p t c u", c=P, u=2)
        for half in range(2):
            pairs_onto_partitions(
                wv_pairs[:, 2 * half : 2 * half + 2, :],
                wv_grouped_pairs[:, 2 * half : 2 * half + 2, :, :],
                in_turn[half],
            )

        def quantise_wv():
            nc.vector.quantize_mx(
                out=wv_codes[:].bitcast(FP8X4), scales=wv_scales[:], in_=wv_grouped[:]
            )

        weight = const.tile([P, SL, H], F32)

        def widen_logw(j):
            first, last = logw_part(j)
            nc.gpsimd.tensor_scalar(
                out=weight[:, first:last, :],
                in0=logw_rows[:, first:last, :H],
                scalar1=1.0,
                scalar2=0.0,
                op0=MULT,
                op1=ADD,
            )

        widen_logw(0)

        wo_grouped = const.tile([P, DO * PACK], BF16, align_bytes=64)
        wo_codes = const.tile([P, DO], U32, align_bytes=64)
        wo_scales = const.tile([P, DO], U8, align_bytes=64)

        def transpose_wo():
            pairs_onto_partitions(
                wo_rows[:].rearrange("p i c -> p (i c)").bitcast(F32).rearrange("p (i w) -> p i w", w=PAIRS),
                wo_grouped[:].bitcast(F32).rearrange("p (i o u) -> p i o u", o=P, u=2),
            )

        def quantise_wo():
            nc.vector.quantize_mx(
                out=wo_codes[:].bitcast(FP8X4),
                scales=wo_scales[:],
                in_=wo_grouped[:],
            )

        grouped_of = {}
        codes_of = {}
        scales_of = {}
        proj_of = {}
        product_of = {}

        def transpose_group(g):
            grouped = work_pool.tile([P, GROUP * BS * PACK], BF16, align_bytes=64)
            src = value_rows[g][:].bitcast(F32).rearrange("b (s w) -> b s w", w=PAIRS)
            dst = grouped[:].bitcast(F32).rearrange("p (s b u) -> p s b u", b=BS, u=2)
            for half in range(GROUP // 2):
                pairs_onto_partitions(
                    src[:, 2 * half : 2 * half + 2, :],
                    dst[:, 2 * half : 2 * half + 2, :, :],
                )
            grouped_of[g] = grouped

        def quantise_group(g):
            codes = work_pool.tile([P, GROUP * BS], U32, align_bytes=64)
            scales = work_pool.tile([P, GROUP * BS], U8, align_bytes=64)
            nc.vector.quantize_mx(
                out=codes[:].bitcast(FP8X4), scales=scales[:], in_=grouped_of[g][:]
            )
            codes_of[g] = codes
            scales_of[g] = scales

        def project_group(g):
            for j in range(GROUP):
                batch = slice(j * BS, (j + 1) * BS)
                proj = proj_pool.tile([P, DP], F32)
                nc.tensor.matmul_mx(
                    out=proj[:],
                    lhsT=codes_of[g][:, batch].bitcast(FP8X4),
                    lhsT_scale=scales_of[g][:, batch],
                    rhs=wv_codes[:].bitcast(FP8X4),
                    rhs_scale=wv_scales[:],
                    start=True,
                    stop=True,
                )
                proj_of[g * GROUP + j] = proj

        attn_part = const.tile([P, DP], F32)
        nc.vector.memset(attn_part[:], 0.0)

        def head_columns(tile, h):
            return tile[:].rearrange("b (t h i) -> b h t i", t=PACK, h=H)[:, h]

        def by_scalar(s):
            return s % SCALAR_EVERY == SCALAR_EVERY - 1

        def by_gpsimd(s):
            return s // SCALAR_EVERY % 2 == 1 and s < SL - LAST_GROUPS * GROUP

        def multiply_group(g):
            for s in range(g * GROUP, (g + 1) * GROUP):
                if not by_scalar(s):
                    continue
                product = prod_pool.tile([P, DP], F32)
                product_of[s] = product
                for h in range(H):
                    nc.scalar.activation(
                        out=head_columns(product, h),
                        in_=head_columns(proj_of[s], h),
                        func=COPY,
                        scale=weight[:, s, h : h + 1],
                    )

        def pool_steps(steps):
            for s in steps:
                if by_scalar(s):
                    continue
                for h in range(H):
                    nc.vector.scalar_tensor_tensor(
                        out=head_columns(attn_part, h),
                        in0=head_columns(proj_of[s], h),
                        scalar=weight[:, s, h : h + 1],
                        in1=head_columns(attn_part, h),
                        op0=MULT,
                        op1=ADD,
                    )

        attn_sum = sum_pool.tile([P, PACK, BS], F32)

        def add_transposed(term, first, last):
            for t in range(PACK):
                nc.tensor.matmul(
                    out=attn_sum[:, t, :],
                    lhsT=term[:, t * P : (t + 1) * P],
                    rhs=ident[:],
                    is_transpose=True,
                    start=first and t == 0,
                    stop=last and t == PACK - 1,
                )

        attn_side = const.tile([P, DP], F32)
        nc.gpsimd.memset(attn_side[:], 0.0)

        def add_products_of_group(g):
            for s in range(g * GROUP, (g + 1) * GROUP):
                if not by_scalar(s):
                    continue
                if not by_gpsimd(s):
                    add_transposed(product_of[s], first=(s == SCALAR_EVERY - 1), last=False)
                else:
                    for t in range(PACK):
                        cols = slice(t * P, (t + 1) * P)
                        nc.gpsimd.tensor_tensor(
                            out=attn_side[:, cols],
                            in0=attn_side[:, cols],
                            in1=product_of[s][:, cols],
                            op=ADD,
                        )

        transpose_group(0)
        quantise_wv()
        quantise_group(0)
        transpose_group(1)
        project_group(0)
        for g in range(2, N_GROUPS + 3):
            pooled = range((g - 2) * GROUP, (g - 1) * GROUP)
            if g % 4 == 2 and (g + 2) // 4 < N_PARTS:
                widen_logw((g + 2) // 4)
            if g < N_GROUPS + 2:
                multiply_group(g - 2)
                if g == 2:
                    pool_steps(pooled[:1])
                    pooled = pooled[1:]
            if g <= N_GROUPS:
                quantise_group(g - 1)
            if g == WO_ROUND + 2:
                quantise_wo()
            if g < N_GROUPS + 2:
                pool_steps(pooled)
            if g == 2:
                transpose_group(g)
            if g + 1 < N_GROUPS:
                transpose_group(g + 1)
            if g >= 3:
                add_products_of_group(g - 3)
            if g == WO_ROUND:
                transpose_wo()
            if g <= N_GROUPS:
                project_group(g - 1)

        add_transposed(attn_side, first=False, last=False)
        add_transposed(attn_part, first=False, last=True)
        attn_grouped = const.tile([P, BS, PACK], BF16, align_bytes=64)
        nc.scalar.copy(out=attn_grouped[:], in_=attn_sum[:].rearrange("p t b -> p b t"))
        attn_codes = const.tile([P, BS], U32, align_bytes=64)
        attn_scales = const.tile([P, BS], U8, align_bytes=64)
        nc.vector.quantize_mx(
            out=attn_codes[:].bitcast(FP8X4),
            scales=attn_scales[:],
            in_=attn_grouped[:].rearrange("p b t -> p (b t)"),
        )
        out_bank = flip_pool.tile([P, DO], F32, tag="flip")
        nc.tensor.matmul_mx(
            out=out_bank[:],
            lhsT=attn_codes[:].bitcast(FP8X4),
            lhsT_scale=attn_scales[:],
            rhs=wo_codes[:].bitcast(FP8X4),
            rhs_scale=wo_scales[:],
            start=True,
            stop=True,
        )
        out_rows = const.tile([P, DO], F32)
        nc.vector.tensor_copy(out=out_rows[:], in_=out_bank[:])
        nc.sync.dma_start(out=out, in_=out_rows[:])
